import numpy as np
import ml_dtypes


def mxq(x, axis, fmt="e4m3"):
    dtype, down = {"e4m3": (ml_dtypes.float8_e4m3fn, 7), "e5m2": (ml_dtypes.float8_e5m2, 14)}[fmt]
    v = np.moveaxis(np.asarray(x, np.float32).astype(ml_dtypes.bfloat16).astype(np.float64), axis, -1)
    blocks = v.reshape(v.shape[:-1] + (-1, 32))
    amax = np.abs(blocks).max(-1, keepdims=True)
    byte = np.maximum(np.where(amax > 0, np.frexp(amax)[1] - 1 + 127, 0) - down, 1)
    scale = np.exp2(byte - 127.0)
    codes = (blocks / scale).astype(np.float32).astype(dtype).astype(np.float64)
    return np.moveaxis((codes * scale).reshape(v.shape), -1, axis)


WIDE = False


def mx_kscale(k):
    if not WIDE:
        return np.ones(k)
    levels = np.array([10, -10, 5, -5, 0])
    a = np.random.permutation(np.resize(levels, k // 512 * 4)).reshape(k // 512, 4)
    idx = np.arange(k)
    return np.exp2(a[idx // 512, idx % 128 // 32])


BF16 = ml_dtypes.bfloat16


def bf(x):
    return np.asarray(x, np.float32).astype(BF16)


def f64(x):
    return np.asarray(x).astype(np.float64)


E2M1 = np.array([0.0, 0.5, 1.0, 1.5, 2.0, 3.0, 4.0, 6.0, -0.0, -0.5, -1.0, -1.5, -2.0, -3.0, -4.0, -6.0])


def pack_weight(w, fmt):
    k, n = w.shape
    w = f64(bf(w)).reshape(k // 32, 32, n)
    amax = np.abs(w).max(1)
    if fmt == "e4m3":
        byte = np.frexp(amax)[1] - 1 + 127 - 7
    else:
        mant, ex = np.frexp(amax / 6.0)
        byte = np.where(mant > 0.5, ex, ex - 1) + 127
    byte = np.clip(np.where(amax > 0, byte, 1), 1, 254)
    scaled = (w * np.exp2(127.0 - byte)[:, None, :]).reshape(k, n).astype(np.float32)
    by_word = np.ascontiguousarray(scaled.reshape(k // 512, 128, 4, n).transpose(0, 1, 3, 2))
    if fmt == "e4m3":
        words = by_word.astype(ml_dtypes.float8_e4m3fn).view(np.uint8)
    else:
        c = by_word.astype(ml_dtypes.float4_e2m1fn).view(np.uint8) & 0xF
        words = c[..., 0::2] | (c[..., 1::2] << 4)
    return np.ascontiguousarray(words), np.ascontiguousarray(byte.astype(np.uint8).reshape(k // 512, 16, n))


def unpack_weight(words, scales, fmt):
    g, p, n, _ = words.shape
    if fmt == "e4m3":
        vals = np.ascontiguousarray(words).view(ml_dtypes.float8_e4m3fn).astype(np.float64)
    else:
        nib = np.empty((g, p, n, 4), np.uint8)
        nib[..., 0::2] = words & 0xF
        nib[..., 1::2] = words >> 4
        vals = E2M1[nib]
    vals = vals * np.repeat(np.exp2(scales.astype(np.float64) - 127.0), 8, axis=1)[..., None]
    return vals.transpose(0, 1, 3, 2).reshape(g * 512, n)


B, D, C = 512, 256, 128
EPS_SQRT = 1e-10
EPS_NORM = 1e-12
FMT = "e4m3"


def setup_inputs():
    s = mx_kscale(D * D)
    a = np.round(np.log2(np.array([s.max(), s.min()])) / 2)
    r = np.repeat(np.exp2(a - a.min()), D // 2)
    g = np.exp2(np.round(np.log2(np.mean(r ** 2))))
    feat = bf(np.random.standard_normal((B, D)) * r ** 2)
    w = np.random.standard_normal((C, D * D)) * g / np.outer(r, r).reshape(-1)
    words, scales = pack_weight(np.ascontiguousarray(w.T), FMT)
    b = bf(np.random.standard_normal(C) * 0.3)
    return {"feat": feat,
            "W_words": words,
            "W_scales": scales,
            "b": b}


def reference(feat, W_words, W_scales, b):
    feat = f64(feat)
    x = (feat[:, :, None] * feat[:, None, :]).reshape(feat.shape[0], -1)
    x = np.sign(x) * np.sqrt(np.abs(x) + EPS_SQRT)
    norm = np.maximum(np.linalg.norm(x, axis=1, keepdims=True), EPS_NORM)
    x = x / norm
    return (mxq(x, 1, "e4m3") @ unpack_weight(W_words, W_scales, FMT)) + f64(b)

@@ -1,0 +1,214 @@
+from contextlib import ExitStack
+
+import concourse.mybir as mybir
+from concourse.masks import make_identity
+
+F32 = mybir.dt.float32
+BF16 = mybir.dt.bfloat16
+U8 = mybir.dt.uint8
+U32 = mybir.dt.uint32
+I32 = mybir.dt.int32
+FP8X4 = mybir.dt.float8_e4m3fn_x4
+ACT = mybir.ActivationFunctionType
+ALU = mybir.AluOpType
+
+P = 128
+B, D, C = 512, 256, 128
+EPS_SQRT = 1e-10
+EPS_NORM = 1e-12
+PACK = 4
+K_PASS = P * PACK
+ROWS = K_PASS // D
+PASSES = D * D // K_PASS
+BLOCKS = B // P
+HALVES = 2
+PAIRS = 2
+W_CHUNK = 16
+
+FLOPS = 2 * B * D * D * C
+
+
+def tile_bcnnresnet_kernel(tc, feat, W_words, W_scales, b, out):
+    nc = tc.nc
+    with ExitStack() as ctx:
+        ctx.enter_context(tc.manual_schedule())
+        const = ctx.enter_context(tc.tile_pool(name="const", bufs=1))
+        roots_pool = ctx.enter_context(tc.tile_pool(name="roots", bufs=3))
+        x_pool = ctx.enter_context(tc.tile_pool(name="x", bufs=2))
+        acc_pool = ctx.enter_context(tc.psum_pool(name="acc", bufs=1))
+        bank_pool = ctx.enter_context(tc.psum_pool(name="banks", bufs=6))
+
+        feat_sb = const.tile([P, BLOCKS, D], BF16)
+        nc.sync.dma_start(out=feat_sb[:], in_=feat.rearrange("(blk p) d -> p blk d", p=P))
+
+        w_scales_sb = const.tile([P, PASSES, C], U8, align_bytes=64)
+        nc.vector.memset(w_scales_sb[:].bitcast(I32), 0)
+        for quad in range(4):
+            nc.sync.dma_start(
+                out=w_scales_sb[32 * quad : 32 * quad + 4].bitcast(I32),
+                in_=W_scales.bitcast(I32)[:, 4 * quad : 4 * quad + 4, :].rearrange("g s c -> s g c"),
+            )
+        w_words_sb = const.tile([P, PASSES, C], U32, align_bytes=64)
+        w_words_dram = W_words.rearrange("g p c t -> g p (c t)").bitcast(I32)
+        for g0 in range(0, PASSES, W_CHUNK):
+            nc.sync.dma_start(
+                out=w_words_sb[:, g0 : g0 + W_CHUNK, :].bitcast(I32),
+                in_=w_words_dram[g0 : g0 + W_CHUNK].rearrange("g p c -> p g c"),
+            )
+        bias_sb = const.tile([P, C], BF16)
+        nc.sync.dma_start(out=bias_sb[:], in_=b.partition_broadcast(P))
+
+        ident = const.tile([P, P], F32)
+        make_identity(nc, ident[:])
+
+        one = const.tile([P, 1], F32)
+        nc.vector.memset(one[:], 1.0)
+        nc.scalar.activation(out=one[:], in_=one[:], func=ACT.Sqrt)
+
+        abs_f = const.tile([P, BLOCKS, D], F32)
+        sum_abs = const.tile([P, BLOCKS], F32)
+        for blk in range(BLOCKS):
+            nc.scalar.activation(
+                out=abs_f[:, blk, :], in_=feat_sb[:, blk, :], func=ACT.Abs, accum_out=sum_abs[:, blk : blk + 1]
+            )
+        abs_by_pair = const.tile([P, BLOCKS, PAIRS, D // PAIRS], BF16)
+        for blk in range(BLOCKS):
+            nc.scalar.activation(
+                out=abs_by_pair[:, blk].rearrange("p u (q e) -> p u q e", e=2),
+                in_=feat_sb[:, blk, :].rearrange("p (q u e) -> p u q e", u=PAIRS, e=2),
+                func=ACT.Abs,
+            )
+
+        nonzero = const.tile([P, BLOCKS, D], BF16)
+        nc.vector.tensor_single_scalar(out=nonzero[:], in_=feat_sb[:], scalar=0.0, op=ALU.not_equal)
+        count = const.tile([P, BLOCKS], F32)
+        nc.vector.tensor_reduce(out=count[:], in_=nonzero[:], axis=mybir.AxisListType.X, op=ALU.add)
+        positive = const.tile([P, BLOCKS, D], BF16)
+        nc.vector.tensor_single_scalar(out=positive[:], in_=feat_sb[:], scalar=0.0, op=ALU.is_gt)
+        negative = const.tile([P, BLOCKS, D], BF16)
+        nc.vector.tensor_single_scalar(out=negative[:], in_=feat_sb[:], scalar=0.0, op=ALU.is_lt)
+        sign = const.tile([P, BLOCKS, D], BF16)
+        nc.vector.tensor_sub(out=sign[:], in0=positive[:], in1=negative[:])
+
+        sum_sq = const.tile([P, BLOCKS], F32)
+        nc.vector.tensor_mul(out=sum_sq[:], in0=sum_abs[:], in1=sum_abs[:])
+        count_sq = const.tile([P, BLOCKS], F32)
+        nc.vector.tensor_mul(out=count_sq[:], in0=count[:], in1=count[:])
+        norm_sq = const.tile([P, BLOCKS], F32)
+        nc.vector.scalar_tensor_tensor(
+            out=norm_sq[:], in0=count_sq[:], scalar=EPS_SQRT, in1=sum_sq[:], op0=ALU.mult, op1=ALU.add
+        )
+        nc.vector.tensor_scalar_max(out=norm_sq[:], in0=norm_sq[:], scalar1=EPS_NORM * EPS_NORM)
+        inv_norm_sq = const.tile([P, BLOCKS], F32)
+        nc.vector.reciprocal(out=inv_norm_sq[:], in_=norm_sq[:])
+        eps_scaled = const.tile([P, BLOCKS], F32)
+        nc.vector.tensor_scalar_mul(out=eps_scaled[:], in0=inv_norm_sq[:], scalar1=EPS_SQRT)
+        row_scale = const.tile([P, BLOCKS, D], F32)
+        for blk in range(BLOCKS):
+            nc.vector.tensor_scalar_mul(
+                out=row_scale[:, blk, :], in0=abs_f[:, blk, :], scalar1=inv_norm_sq[:, blk : blk + 1]
+            )
+
+        def square_roots(g):
+            roots = roots_pool.tile([P, BLOCKS, PAIRS, ROWS, D // PAIRS], BF16)
+            for blk in range(BLOCKS):
+                for r in range(ROWS):
+                    i = ROWS * g + r
+                    nc.scalar.activation(
+                        out=roots[:, blk, :, r, :],
+                        in_=abs_by_pair[:, blk],
+                        func=ACT.Sqrt,
+                        scale=row_scale[:, blk, i : i + 1],
+                        bias=eps_scaled[:, blk : blk + 1],
+                    )
+            return roots
+
+        def apply_row_signs(g, roots):
+            for blk in range(BLOCKS):
+                for r in range(ROWS):
+                    i = ROWS * g + r
+                    nc.vector.tensor_scalar_mul(
+                        out=roots[:, blk, :, r, :], in0=roots[:, blk, :, r, :], scalar1=sign[:, blk, i : i + 1]
+                    )
+
+        def transpose_words(roots):
+            banks = []
+            for h in range(HALVES):
+                bank = bank_pool.tile([P, PAIRS, B // HALVES], F32)
+                for half_blk in range(BLOCKS // HALVES):
+                    blk = h * (BLOCKS // HALVES) + half_blk
+                    for u in range(PAIRS):
+                        nc.tensor.transpose(
+                            out=bank[:, u, half_blk * P : (half_blk + 1) * P],
+                            in_=roots[:, blk, u].rearrange("p r w -> p (r w)").bitcast(F32),
+                            identity=ident[:],
+                        )
+                banks.append(bank)
+            return banks
+
+        def words_in_order(bank):
+            return bank[:].bitcast(BF16).rearrange("p u (n e) -> p n u e", e=2)
+
+        def half_of(columns, h):
+            width = B // HALVES * PACK
+            return columns[:, h * width : (h + 1) * width].rearrange("p (n u e) -> p n u e", u=PAIRS, e=2)
+
+        sign_rows = const.tile([P, BLOCKS, PAIRS, ROWS, D // PAIRS], BF16)
+        for r in range(ROWS):
+            nc.vector.tensor_copy(
+                out=sign_rows[:, :, :, r, :].rearrange("p blk u (q e) -> p blk u q e", e=2),
+                in_=sign[:].rearrange("p blk (q u e) -> p blk u q e", u=PAIRS, e=2),
+            )
+        column_sign = const.tile([P, B * PACK], BF16)
+        sign_banks = transpose_words(sign_rows)
+        for h in range(HALVES):
+            nc.vector.tensor_copy(out=half_of(column_sign, h), in_=words_in_order(sign_banks[h]))
+
+        acc = acc_pool.tile([C, B], F32)
+
+        def leave_psum(banks):
+            x_bf16 = x_pool.tile([P, B * PACK], BF16, align_bytes=64)
+            for h in range(HALVES):
+                nc.vector.tensor_tensor(
+                    out=half_of(x_bf16, h), in0=words_in_order(banks[h]), in1=half_of(column_sign, h), op=ALU.mult
+                )
+            return x_bf16
+
+        def quantise_and_multiply(g, x_bf16):
+            x_words = x_pool.tile([P, B], U32, align_bytes=64)
+            x_scales = x_pool.tile([P, B], U8, align_bytes=64)
+            nc.vector.quantize_mx(out=x_words[:].bitcast(FP8X4), scales=x_scales[:], in_=x_bf16[:])
+            nc.tensor.matmul_mx(
+                out=acc[:],
+                lhsT=w_words_sb[:, g, :].bitcast(FP8X4),
+                lhsT_scale=w_scales_sb[:, g, :],
+                rhs=x_words[:].bitcast(FP8X4),
+                rhs_scale=x_scales[:],
+                start=(g == 0),
+                stop=(g == PASSES - 1),
+            )
+
+        roots_of = {}
+        banks_of = {}
+        for step in range(PASSES + 2):
+            if step >= 2:
+                x_bf16 = leave_psum(banks_of[step - 2])
+            if step < PASSES:
+                roots_of[step] = square_roots(step)
+            if 1 <= step <= PASSES:
+                signed = roots_of[step - 1]
+                apply_row_signs(step - 1, signed)
+                banks_of[step - 1] = transpose_words(signed)
+            if step >= 2:
+                quantise_and_multiply(step - 2, x_bf16)
+
+        acc_sb = const.tile([C, B], F32)
+        nc.vector.tensor_copy(out=acc_sb[:], in_=acc[:])
+        out_ps = bank_pool.tile([P, BLOCKS, C], F32, tag="bank")
+        for blk in range(BLOCKS):
+            nc.tensor.transpose(out=out_ps[:, blk, :], in_=acc_sb[:, blk * P : (blk + 1) * P], identity=ident[:])
+        out_sb = const.tile([P, BLOCKS, C], F32)
+        nc.vector.tensor_tensor(
+            out=out_sb[:], in0=out_ps[:], in1=bias_sb[:].unsqueeze(1).to_broadcast([P, BLOCKS, C]), op=ALU.add
+        )
+        nc.sync.dma_start(out=out.rearrange("(blk p) c -> p blk c", p=P), in_=out_sb[:])

@@ -190,17 +190,17 @@ def tile_bcnnresnet_kernel(tc, feat, W_words, W_scales, b, out):
 
         roots_of = {}
         banks_of = {}
-        for step in range(PASSES + 2):
-            if step >= 2:
-                x_bf16 = leave_psum(banks_of[step - 2])
+        x_of = {}
+        for step in range(PASSES + 3):
             if step < PASSES:
                 roots_of[step] = square_roots(step)
             if 1 <= step <= PASSES:
-                signed = roots_of[step - 1]
-                apply_row_signs(step - 1, signed)
-                banks_of[step - 1] = transpose_words(signed)
-            if step >= 2:
-                quantise_and_multiply(step - 2, x_bf16)
+                apply_row_signs(step - 1, roots_of[step - 1])
+                banks_of[step - 1] = transpose_words(roots_of[step - 1])
+            if step >= 3:
+                quantise_and_multiply(step - 3, x_of[step - 3])
+            if 2 <= step <= PASSES + 1:
+                x_of[step - 2] = leave_psum(banks_of[step - 2])
 
         acc_sb = const.tile([C, B], F32)
         nc.vector.tensor_copy(out=acc_sb[:], in_=acc[:])

@@ -127,9 +127,14 @@ def tile_bcnnresnet_kernel(tc, feat, W_words, W_scales, b, out):
             for blk in range(BLOCKS):
                 for r in range(ROWS):
                     i = ROWS * g + r
-                    nc.vector.tensor_scalar_mul(
-                        out=roots[:, blk, :, r, :], in0=roots[:, blk, :, r, :], scalar1=sign[:, blk, i : i + 1]
-                    )
+                    values = roots[:, blk, :, r, :]
+                    if blk < BLOCKS - 1:
+                        nc.vector.tensor_scalar_mul(out=values, in0=values, scalar1=sign[:, blk, i : i + 1])
+                    else:
+                        nc.gpsimd.tensor_scalar(
+                            out=values, in0=values, scalar1=sign[:, blk, i : i + 1], scalar2=0.0,
+                            op0=ALU.mult, op1=ALU.add,
+                        )
 
         def transpose_words(roots):
             banks = []

@@ -24,6 +24,7 @@ BLOCKS = B // P
 HALVES = 2
 PAIRS = 2
 W_CHUNK = 16
+BANK = 512
 
 FLOPS = 2 * B * D * D * C
 
@@ -36,7 +37,7 @@ def tile_bcnnresnet_kernel(tc, feat, W_words, W_scales, b, out):
         roots_pool = ctx.enter_context(tc.tile_pool(name="roots", bufs=3))
         x_pool = ctx.enter_context(tc.tile_pool(name="x", bufs=2))
         acc_pool = ctx.enter_context(tc.psum_pool(name="acc", bufs=1))
-        bank_pool = ctx.enter_context(tc.psum_pool(name="banks", bufs=6))
+        bank_pool = ctx.enter_context(tc.psum_pool(name="banks", bufs=4))
 
         feat_sb = const.tile([P, BLOCKS, D], BF16)
         nc.sync.dma_start(out=feat_sb[:], in_=feat.rearrange("(blk p) d -> p blk d", p=P))
@@ -128,7 +129,7 @@ def tile_bcnnresnet_kernel(tc, feat, W_words, W_scales, b, out):
                 for r in range(ROWS):
                     i = ROWS * g + r
                     values = roots[:, blk, :, r, :]
-                    if blk < BLOCKS - 1:
+                    if blk < BLOCKS - 1 or g == PASSES - 1:
                         nc.vector.tensor_scalar_mul(out=values, in0=values, scalar1=sign[:, blk, i : i + 1])
                     else:
                         nc.gpsimd.tensor_scalar(
@@ -169,7 +170,7 @@ def tile_bcnnresnet_kernel(tc, feat, W_words, W_scales, b, out):
         for h in range(HALVES):
             nc.vector.tensor_copy(out=half_of(column_sign, h), in_=words_in_order(sign_banks[h]))
 
-        acc = acc_pool.tile([C, B], F32)
+        acc = [acc_pool.tile([P, BANK], F32, name="acc%d" % blk) for blk in range(BLOCKS)]
 
         def leave_psum(banks):
             x_bf16 = x_pool.tile([P, B * PACK], BF16, align_bytes=64)
@@ -183,15 +184,17 @@ def tile_bcnnresnet_kernel(tc, feat, W_words, W_scales, b, out):
             x_words = x_pool.tile([P, B], U32, align_bytes=64)
             x_scales = x_pool.tile([P, B], U8, align_bytes=64)
             nc.vector.quantize_mx(out=x_words[:].bitcast(FP8X4), scales=x_scales[:], in_=x_bf16[:])
-            nc.tensor.matmul_mx(
-                out=acc[:],
-                lhsT=w_words_sb[:, g, :].bitcast(FP8X4),
-                lhsT_scale=w_scales_sb[:, g, :],
-                rhs=x_words[:].bitcast(FP8X4),
-                rhs_scale=x_scales[:],
-                start=(g == 0),
-                stop=(g == PASSES - 1),
-            )
+            for blk in range(BLOCKS):
+                samples = slice(blk * P, (blk + 1) * P)
+                nc.tensor.matmul_mx(
+                    out=acc[blk][:, :C],
+                    lhsT=x_words[:, samples].bitcast(FP8X4),
+                    lhsT_scale=x_scales[:, samples],
+                    rhs=w_words_sb[:, g, :].bitcast(FP8X4),
+                    rhs_scale=w_scales_sb[:, g, :],
+                    start=(g == 0),
+                    stop=(g == PASSES - 1),
+                )
 
         roots_of = {}
         banks_of = {}
@@ -207,13 +210,7 @@ def tile_bcnnresnet_kernel(tc, feat, W_words, W_scales, b, out):
             if 2 <= step <= PASSES + 1:
                 x_of[step - 2] = leave_psum(banks_of[step - 2])
 
-        acc_sb = const.tile([C, B], F32)
-        nc.vector.tensor_copy(out=acc_sb[:], in_=acc[:])
-        out_ps = bank_pool.tile([P, BLOCKS, C], F32, tag="bank")
-        for blk in range(BLOCKS):
-            nc.tensor.transpose(out=out_ps[:, blk, :], in_=acc_sb[:, blk * P : (blk + 1) * P], identity=ident[:])
         out_sb = const.tile([P, BLOCKS, C], F32)
-        nc.vector.tensor_tensor(
-            out=out_sb[:], in0=out_ps[:], in1=bias_sb[:].unsqueeze(1).to_broadcast([P, BLOCKS, C]), op=ALU.add
-        )
+        for blk in range(BLOCKS):
+            nc.vector.tensor_tensor(out=out_sb[:, blk, :], in0=acc[blk][:, :C], in1=bias_sb[:], op=ALU.add)
         nc.sync.dma_start(out=out.rearrange("(blk p) c -> p blk c", p=P), in_=out_sb[:])

@@ -24,6 +24,8 @@ BLOCKS = B // P
 HALVES = 2
 PAIRS = 2
 W_CHUNK = 16
+KEPT = 8
+MIRRORED = ROWS * KEPT // PAIRS
 BANK = 512
 
 FLOPS = 2 * B * D * D * C
@@ -110,19 +112,31 @@ def tile_bcnnresnet_kernel(tc, feat, W_words, W_scales, b, out):
                 out=row_scale[:, blk, :], in0=abs_f[:, blk, :], scalar1=inv_norm_sq[:, blk : blk + 1]
             )
 
+        kept = const.tile([P, PAIRS, MIRRORED, PAIRS, D // PAIRS], BF16)
+
+        def kept_row(i):
+            return kept[:, (i // 2) % PAIRS, 2 * (i // PACK) + i % 2]
+
         def square_roots(g):
             roots = roots_pool.tile([P, BLOCKS, PAIRS, ROWS, D // PAIRS], BF16)
             for blk in range(BLOCKS):
+                first = MIRRORED if (blk == 0 and g >= KEPT) else 0
                 for r in range(ROWS):
                     i = ROWS * g + r
                     nc.scalar.activation(
-                        out=roots[:, blk, :, r, :],
-                        in_=abs_by_pair[:, blk],
+                        out=kept_row(i) if (blk == 0 and g < KEPT) else roots[:, blk, :, r, first:],
+                        in_=abs_by_pair[:, blk, :, first:],
                         func=ACT.Sqrt,
                         scale=row_scale[:, blk, i : i + 1],
                         bias=eps_scaled[:, blk : blk + 1],
                     )
             return roots
+
+        def mirror(g, roots):
+            nc.vector.tensor_copy(
+                out=roots[:, 0, :, :, :MIRRORED],
+                in_=kept[:, :, :, g % PAIRS, ROWS * (g // PAIRS) : ROWS * (g // PAIRS) + ROWS].rearrange("p u j r -> p u r j"),
+            )
 
         def apply_row_signs(g, roots):
             for blk in range(BLOCKS):
@@ -130,7 +144,8 @@ def tile_bcnnresnet_kernel(tc, feat, W_words, W_scales, b, out):
                     i = ROWS * g + r
                     values = roots[:, blk, :, r, :]
                     if blk < BLOCKS - 1 or g == PASSES - 1:
-                        nc.vector.tensor_scalar_mul(out=values, in0=values, scalar1=sign[:, blk, i : i + 1])
+                        unsigned = kept_row(i) if (blk == 0 and g < KEPT) else values
+                        nc.vector.tensor_scalar_mul(out=values, in0=unsigned, scalar1=sign[:, blk, i : i + 1])
                     else:
                         nc.gpsimd.tensor_scalar(
                             out=values, in0=values, scalar1=sign[:, blk, i : i + 1], scalar2=0.0,
@@ -207,6 +222,8 @@ def tile_bcnnresnet_kernel(tc, feat, W_words, W_scales, b, out):
                 banks_of[step - 1] = transpose_words(roots_of[step - 1])
             if step >= 3:
                 quantise_and_multiply(step - 3, x_of[step - 3])
+            if KEPT <= step < PASSES:
+                mirror(step, roots_of[step])
             if 2 <= step <= PASSES + 1:
                 x_of[step - 2] = leave_psum(banks_of[step - 2])
 

from contextlib import ExitStack

import concourse.mybir as mybir
from concourse.masks import make_identity

F32 = mybir.dt.float32
BF16 = mybir.dt.bfloat16
U8 = mybir.dt.uint8
U32 = mybir.dt.uint32
I32 = mybir.dt.int32
FP8X4 = mybir.dt.float8_e4m3fn_x4
ACT = mybir.ActivationFunctionType
ALU = mybir.AluOpType

P = 128
B, D, C = 512, 256, 128
EPS_SQRT = 1e-10
EPS_NORM = 1e-12
PACK = 4
K_PASS = P * PACK
ROWS = K_PASS // D
PASSES = D * D // K_PASS
BLOCKS = B // P
HALVES = 2
PAIRS = 2
W_CHUNK = 16
KEPT = 8
MIRRORED = ROWS * KEPT // PAIRS
BANK = 512

FLOPS = 2 * B * D * D * C


def tile_bcnnresnet_kernel(tc, feat, W_words, W_scales, b, out):
    nc = tc.nc
    with ExitStack() as ctx:
        ctx.enter_context(tc.manual_schedule())
        const = ctx.enter_context(tc.tile_pool(name="const", bufs=1))
        roots_pool = ctx.enter_context(tc.tile_pool(name="roots", bufs=3))
        x_pool = ctx.enter_context(tc.tile_pool(name="x", bufs=2))
        acc_pool = ctx.enter_context(tc.psum_pool(name="acc", bufs=1))
        bank_pool = ctx.enter_context(tc.psum_pool(name="banks", bufs=4))

        feat_sb = const.tile([P, BLOCKS, D], BF16)
        nc.sync.dma_start(out=feat_sb[:], in_=feat.rearrange("(blk p) d -> p blk d", p=P))

        w_scales_sb = const.tile([P, PASSES, C], U8, align_bytes=64)
        nc.vector.memset(w_scales_sb[:].bitcast(I32), 0)
        for quad in range(4):
            nc.sync.dma_start(
                out=w_scales_sb[32 * quad : 32 * quad + 4].bitcast(I32),
                in_=W_scales.bitcast(I32)[:, 4 * quad : 4 * quad + 4, :].rearrange("g s c -> s g c"),
            )
        w_words_sb = const.tile([P, PASSES, C], U32, align_bytes=64)
        w_words_dram = W_words.rearrange("g p c t -> g p (c t)").bitcast(I32)
        for g0 in range(0, PASSES, W_CHUNK):
            nc.sync.dma_start(
                out=w_words_sb[:, g0 : g0 + W_CHUNK, :].bitcast(I32),
                in_=w_words_dram[g0 : g0 + W_CHUNK].rearrange("g p c -> p g c"),
            )
        bias_sb = const.tile([P, C], BF16)
        nc.sync.dma_start(out=bias_sb[:], in_=b.partition_broadcast(P))

        ident = const.tile([P, P], F32)
        make_identity(nc, ident[:])

        one = const.tile([P, 1], F32)
        nc.vector.memset(one[:], 1.0)
        nc.scalar.activation(out=one[:], in_=one[:], func=ACT.Sqrt)

        abs_f = const.tile([P, BLOCKS, D], F32)
        sum_abs = const.tile([P, BLOCKS], F32)
        for blk in range(BLOCKS):
            nc.scalar.activation(
                out=abs_f[:, blk, :], in_=feat_sb[:, blk, :], func=ACT.Abs, accum_out=sum_abs[:, blk : blk + 1]
            )
        abs_by_pair = const.tile([P, BLOCKS, PAIRS, D // PAIRS], BF16)
        for blk in range(BLOCKS):
            nc.scalar.activation(
                out=abs_by_pair[:, blk].rearrange("p u (q e) -> p u q e", e=2),
                in_=feat_sb[:, blk, :].rearrange("p (q u e) -> p u q e", u=PAIRS, e=2),
                func=ACT.Abs,
            )

        nonzero = const.tile([P, BLOCKS, D], BF16)
        nc.vector.tensor_single_scalar(out=nonzero[:], in_=feat_sb[:], scalar=0.0, op=ALU.not_equal)
        count = const.tile([P, BLOCKS], F32)
        nc.vector.tensor_reduce(out=count[:], in_=nonzero[:], axis=mybir.AxisListType.X, op=ALU.add)
        positive = const.tile([P, BLOCKS, D], BF16)
        nc.vector.tensor_single_scalar(out=positive[:], in_=feat_sb[:], scalar=0.0, op=ALU.is_gt)
        negative = const.tile([P, BLOCKS, D], BF16)
        nc.vector.tensor_single_scalar(out=negative[:], in_=feat_sb[:], scalar=0.0, op=ALU.is_lt)
        sign = const.tile([P, BLOCKS, D], BF16)
        nc.vector.tensor_sub(out=sign[:], in0=positive[:], in1=negative[:])

        sum_sq = const.tile([P, BLOCKS], F32)
        nc.vector.tensor_mul(out=sum_sq[:], in0=sum_abs[:], in1=sum_abs[:])
        count_sq = const.tile([P, BLOCKS], F32)
        nc.vector.tensor_mul(out=count_sq[:], in0=count[:], in1=count[:])
        norm_sq = const.tile([P, BLOCKS], F32)
        nc.vector.scalar_tensor_tensor(
            out=norm_sq[:], in0=count_sq[:], scalar=EPS_SQRT, in1=sum_sq[:], op0=ALU.mult, op1=ALU.add
        )
        nc.vector.tensor_scalar_max(out=norm_sq[:], in0=norm_sq[:], scalar1=EPS_NORM * EPS_NORM)
        inv_norm_sq = const.tile([P, BLOCKS], F32)
        nc.vector.reciprocal(out=inv_norm_sq[:], in_=norm_sq[:])
        eps_scaled = const.tile([P, BLOCKS], F32)
        nc.vector.tensor_scalar_mul(out=eps_scaled[:], in0=inv_norm_sq[:], scalar1=EPS_SQRT)
        row_scale = const.tile([P, BLOCKS, D], F32)
        for blk in range(BLOCKS):
            nc.vector.tensor_scalar_mul(
                out=row_scale[:, blk, :], in0=abs_f[:, blk, :], scalar1=inv_norm_sq[:, blk : blk + 1]
            )

        kept = const.tile([P, PAIRS, MIRRORED, PAIRS, D // PAIRS], BF16)

        def kept_row(i):
            return kept[:, (i // 2) % PAIRS, 2 * (i // PACK) + i % 2]

        def square_roots(g):
            roots = roots_pool.tile([P, BLOCKS, PAIRS, ROWS, D // PAIRS], BF16)
            for blk in range(BLOCKS):
                first = MIRRORED if (blk == 0 and g >= KEPT) else 0
                for r in range(ROWS):
                    i = ROWS * g + r
                    nc.scalar.activation(
                        out=kept_row(i) if (blk == 0 and g < KEPT) else roots[:, blk, :, r, first:],
                        in_=abs_by_pair[:, blk, :, first:],
                        func=ACT.Sqrt,
                        scale=row_scale[:, blk, i : i + 1],
                        bias=eps_scaled[:, blk : blk + 1],
                    )
            return roots

        def mirror(g, roots):
            nc.vector.tensor_copy(
                out=roots[:, 0, :, :, :MIRRORED],
                in_=kept[:, :, :, g % PAIRS, ROWS * (g // PAIRS) : ROWS * (g // PAIRS) + ROWS].rearrange("p u j r -> p u r j"),
            )

        def apply_row_signs(g, roots):
            for blk in range(BLOCKS):
                for r in range(ROWS):
                    i = ROWS * g + r
                    values = roots[:, blk, :, r, :]
                    if blk < BLOCKS - 1 or g == PASSES - 1:
                        unsigned = kept_row(i) if (blk == 0 and g < KEPT) else values
                        nc.vector.tensor_scalar_mul(out=values, in0=unsigned, scalar1=sign[:, blk, i : i + 1])
                    else:
                        nc.gpsimd.tensor_scalar(
                            out=values, in0=values, scalar1=sign[:, blk, i : i + 1], scalar2=0.0,
                            op0=ALU.mult, op1=ALU.add,
                        )

        def transpose_words(roots):
            banks = []
            for h in range(HALVES):
                bank = bank_pool.tile([P, PAIRS, B // HALVES], F32)
                for half_blk in range(BLOCKS // HALVES):
                    blk = h * (BLOCKS // HALVES) + half_blk
                    for u in range(PAIRS):
                        nc.tensor.transpose(
                            out=bank[:, u, half_blk * P : (half_blk + 1) * P],
                            in_=roots[:, blk, u].rearrange("p r w -> p (r w)").bitcast(F32),
                            identity=ident[:],
                        )
                banks.append(bank)
            return banks

        def words_in_order(bank):
            return bank[:].bitcast(BF16).rearrange("p u (n e) -> p n u e", e=2)

        def half_of(columns, h):
            width = B // HALVES * PACK
            return columns[:, h * width : (h + 1) * width].rearrange("p (n u e) -> p n u e", u=PAIRS, e=2)

        sign_rows = const.tile([P, BLOCKS, PAIRS, ROWS, D // PAIRS], BF16)
        for r in range(ROWS):
            nc.vector.tensor_copy(
                out=sign_rows[:, :, :, r, :].rearrange("p blk u (q e) -> p blk u q e", e=2),
                in_=sign[:].rearrange("p blk (q u e) -> p blk u q e", u=PAIRS, e=2),
            )
        column_sign = const.tile([P, B * PACK], BF16)
        sign_banks = transpose_words(sign_rows)
        for h in range(HALVES):
            nc.vector.tensor_copy(out=half_of(column_sign, h), in_=words_in_order(sign_banks[h]))

        acc = [acc_pool.tile([P, BANK], F32, name="acc%d" % blk) for blk in range(BLOCKS)]

        def leave_psum(banks):
            x_bf16 = x_pool.tile([P, B * PACK], BF16, align_bytes=64)
            for h in range(HALVES):
                nc.vector.tensor_tensor(
                    out=half_of(x_bf16, h), in0=words_in_order(banks[h]), in1=half_of(column_sign, h), op=ALU.mult
                )
            return x_bf16

        def quantise_and_multiply(g, x_bf16):
            x_words = x_pool.tile([P, B], U32, align_bytes=64)
            x_scales = x_pool.tile([P, B], U8, align_bytes=64)
            nc.vector.quantize_mx(out=x_words[:].bitcast(FP8X4), scales=x_scales[:], in_=x_bf16[:])
            for blk in range(BLOCKS):
                samples = slice(blk * P, (blk + 1) * P)
                nc.tensor.matmul_mx(
                    out=acc[blk][:, :C],
                    lhsT=x_words[:, samples].bitcast(FP8X4),
                    lhsT_scale=x_scales[:, samples],
                    rhs=w_words_sb[:, g, :].bitcast(FP8X4),
                    rhs_scale=w_scales_sb[:, g, :],
                    start=(g == 0),
                    stop=(g == PASSES - 1),
                )

        roots_of = {}
        banks_of = {}
        x_of = {}
        for step in range(PASSES + 3):
            if step < PASSES:
                roots_of[step] = square_roots(step)
            if 1 <= step <= PASSES:
                apply_row_signs(step - 1, roots_of[step - 1])
                banks_of[step - 1] = transpose_words(roots_of[step - 1])
            if step >= 3:
                quantise_and_multiply(step - 3, x_of[step - 3])
            if KEPT <= step < PASSES:
                mirror(step, roots_of[step])
            if 2 <= step <= PASSES + 1:
                x_of[step - 2] = leave_psum(banks_of[step - 2])

        out_sb = const.tile([P, BLOCKS, C], F32)
        for blk in range(BLOCKS):
            nc.vector.tensor_tensor(out=out_sb[:, blk, :], in0=acc[blk][:, :C], in1=bias_sb[:], op=ALU.add)
        nc.sync.dma_start(out=out.rearrange("(blk p) c -> p blk c", p=P), in_=out_sb[:])
